import numpy as np
import ml_dtypes


def mxq(x, axis, fmt="e4m3"):
    dtype, down = {"e4m3": (ml_dtypes.float8_e4m3fn, 7), "e5m2": (ml_dtypes.float8_e5m2, 14)}[fmt]
    v = np.moveaxis(np.asarray(x, np.float32).astype(ml_dtypes.bfloat16).astype(np.float64), axis, -1)
    blocks = v.reshape(v.shape[:-1] + (-1, 32))
    amax = np.abs(blocks).max(-1, keepdims=True)
    byte = np.maximum(np.where(amax > 0, np.frexp(amax)[1] - 1 + 127, 0) - down, 1)
    scale = np.exp2(byte - 127.0)
    codes = (blocks / scale).astype(np.float32).astype(dtype).astype(np.float64)
    return np.moveaxis((codes * scale).reshape(v.shape), -1, axis)


WIDE = False


def mx_kscale(k):
    if not WIDE:
        return np.ones(k)
    levels = np.array([10, -10, 5, -5, 0])
    if k % 512:
        return np.exp2(np.random.permutation(np.resize(levels, k // 32))).repeat(32)
    a = np.empty((k // 512, 16))
    for p in range(k // 512):
        a[p, :8] = np.random.permutation(np.resize(levels, 8))
        for g in range(8):
            far = levels[np.abs(levels - a[p, g]) >= 10]
            a[p, g + 8] = far[np.random.randint(len(far))]
    return np.exp2(a.ravel()).repeat(32)


BF16 = ml_dtypes.bfloat16


def bf(x):
    return np.asarray(x, np.float32).astype(BF16)


def f64(x):
    return np.asarray(x).astype(np.float64)


B, C, CK, CV, CO, H, W, P1, P2, P3, P4 = 1, 1024, 256, 256, 1024, 24, 48, 1, 3, 6, 8
PSP_SIZES = (P1, P2, P3, P4)
EPS = 1e-5
N = H * W


def bnrelu(x, gamma, beta, mean, var):
    inv = 1.0 / np.sqrt(var + EPS)
    return np.maximum((x - mean[None, :, None]) * (inv * gamma)[None, :, None] + beta[None, :, None], 0.0)


def psp(x):
    b, c = x.shape[:2]
    outs = []
    for s in PSP_SIZES:
        outs.append(x.reshape(b, c, s, H // s, s, W // s).mean(axis=(3, 5)).reshape(b, c, s * s))
    return np.concatenate(outs, axis=-1)


def draw0():
    s = mx_kscale(C)
    fine = np.random.standard_normal((B, C, H, W))
    coarse = np.random.standard_normal((B, C, P4, P4))
    coarse = np.repeat(np.repeat(coarse, H // P4, axis=2), W // P4, axis=3)
    return {"feats": bf((fine + coarse) * np.sqrt(0.5) * s[None, :, None, None]),
            "Wk": bf(np.random.standard_normal((CK, C)) * 1.5 / np.sqrt(C) / s[None, :]),
            "bk": bf(np.random.standard_normal(CK) * 0.2),
            "gk": bf(1.0 + 0.1 * np.random.standard_normal(CK)),
            "betak": bf(np.random.standard_normal(CK) * 0.2),
            "mk": bf(np.random.standard_normal(CK) * 0.2),
            "vk": bf(np.random.uniform(0.5, 1.5, CK)),
            "Wv": bf(np.random.standard_normal((CV, C)) / np.sqrt(C) / s[None, :]),
            "bv": bf(np.random.standard_normal(CV) * 0.2)}


def core(feats, Wk, bk, gk, betak, mk, vk, Wv, bv):
    xq = mxq(f64(feats).reshape(B, C, N), 1, "e4m3")
    pre = (mxq(f64(Wk), 1, "e4m3") @ xq) + f64(bk)[None, :, None]
    kf = bnrelu(pre, f64(gk), f64(betak), f64(mk), f64(vk)).reshape(B, CK, H, W)
    keyp = psp(kf)
    val = ((mxq(f64(Wv), 1, "e4m3") @ xq) + f64(bv)[None, :, None]).reshape(B, CV, H, W)
    value = psp(val).transpose(0, 2, 1)
    return kf, keyp, value


def e4m3fn_bytes(y):
    return np.clip(np.asarray(y, np.float64), -448.0, 448.0).astype(np.float32).astype(ml_dtypes.float8_e4m3fn).view(np.uint8)


def e4m3fn_values(b):
    return np.asarray(b, np.uint8).view(ml_dtypes.float8_e4m3fn).astype(np.float64)


def setup_inputs():
    d = draw0()
    x0 = np.asarray(d['feats']).astype(np.float64)
    s = (np.max(np.abs(x0), axis=(0, 2, 3), keepdims=True) / 448.0).astype(np.float32)
    out = {}
    for k, v in d.items():
        if k == 'feats':
            out['feats_bytes'] = e4m3fn_bytes(x0 / s.astype(np.float64))
            out['feats_scale'] = s
        else:
            out[k] = v
    return out


def reference(feats_bytes, feats_scale, Wk, bk, gk, betak, mk, vk, Wv, bv):
    return core(e4m3fn_values(feats_bytes) * feats_scale.astype(np.float64), Wk, bk, gk, betak, mk, vk, Wv, bv)

@@ -1,0 +1,419 @@
+from contextlib import ExitStack
+
+import concourse.mybir as mybir
+from concourse.masks import make_identity
+
+F32 = mybir.dt.float32
+BF16 = mybir.dt.bfloat16
+U32 = mybir.dt.uint32
+U8 = mybir.dt.uint8
+FP8 = mybir.dt.float8_e4m3fn
+FP8X4 = mybir.dt.float8_e4m3fn_x4
+ALU = mybir.AluOpType
+ACT = mybir.ActivationFunctionType
+AX = mybir.AxisListType
+
+P = 128
+NPOS = 1152
+EPS = 1e-5
+FLOPS = 2 * 512 * 1024 * 1152
+
+PIECES = ((0, 512), (512, 640))
+CHUNKS = ((0, 512, True, 0, 0), (512, 512, True, 1, 0), (1024, 128, False, 1, 512))
+ALL4 = (0, 1, 2, 3)
+
+
+def tile_apnb_pa_kernel(tc, feats_bytes, feats_scale, Wk, bk, gk, betak, mk, vk, Wv, bv, out_0, out_1, out_2):
+    nc = tc.nc
+    with ExitStack() as ctx:
+        keep = ctx.enter_context(tc.tile_pool(name="keep", bufs=1))
+        ps_big = ctx.enter_context(tc.psum_pool(name="ps_big", bufs=4))
+        ps_vt = ctx.enter_context(tc.psum_pool(name="ps_vt", bufs=3))
+        ps_val = ctx.enter_context(tc.psum_pool(name="ps_val", bufs=1))
+        ctx.enter_context(tc.manual_schedule())
+
+        fb = feats_bytes[0].rearrange("(g p t) h w -> g p t (h w)", g=2, p=P, t=4)
+        sc = keep.tile([P, 2, 4], F32, name="sc")
+        nc.sync.dma_start(out=sc[:], in_=feats_scale[0].rearrange("(g p t) a b -> p g (t a b)", g=2, p=P, t=4))
+        xb = [keep.tile([P, 2, 4, w], U8, name="xb%d" % i) for i, (c0, w) in enumerate(PIECES)]
+
+        def load_bytes(i):
+            c0, w = PIECES[i]
+            for g in range(2):
+                nc.sync.dma_start(out=xb[i][:, g], in_=fb[g][:, :, c0 : c0 + w])
+
+        load_bytes(0)
+        wk_sb = keep.tile([P, 2, 1024], BF16, name="wk_sb")
+        nc.sync.dma_start(out=wk_sb[:], in_=Wk.rearrange("(p m) k -> p m k", m=2))
+        wv_sb = keep.tile([P, 2, 1024], BF16, name="wv_sb")
+        nc.sync.dma_start(out=wv_sb[:], in_=Wv.rearrange("(r p) k -> p r k", r=2))
+        load_bytes(1)
+        bn_in = {}
+        for nm, vec in (("vk", vk), ("gk", gk), ("bk", bk), ("mk", mk), ("betak", betak)):
+            bn_in[nm] = keep.tile([P, 2], BF16, name="bn_" + nm)
+            nc.sync.dma_start(out=bn_in[nm][:], in_=vec.rearrange("(p m) -> p m", m=2))
+        bv_sb = keep.tile([P, 256], BF16, name="bv_sb")
+        nc.sync.dma_start(out=bv_sb[0:1, :], in_=bv.rearrange("(o c) -> o c", o=1))
+
+        dummy = keep.tile([P, 2], F32, name="dummy")
+        nc.gpsimd.memset(dummy[:, 0:1], 1.0)
+        nc.scalar.activation(out=dummy[:, 1:2], in_=dummy[:, 0:1], func=ACT.Sqrt)
+        nn = keep.tile([P, 5], F32, name="nn")
+        nc.gpsimd.iota(nn[:, 0:4], pattern=[[256, 4]], base=0, channel_multiplier=2, allow_small_or_imprecise_dtypes=True)
+        nc.gpsimd.iota(nn[:, 4:5], pattern=[[0, 1]], base=1024, channel_multiplier=1, allow_small_or_imprecise_dtypes=True)
+        th24 = keep.tile([P, 23], F32, name="th24")
+        nc.gpsimd.iota(th24[:], pattern=[[24, 23]], base=24, channel_multiplier=0, allow_small_or_imprecise_dtypes=True)
+        thr = keep.tile([P, 20], F32, name="thr")
+        nc.gpsimd.iota(thr[:, 0:9], pattern=[[3, 9]], base=0, channel_multiplier=0, allow_small_or_imprecise_dtypes=True)
+        nc.gpsimd.iota(thr[:, 9:16], pattern=[[4, 7]], base=0, channel_multiplier=0, allow_small_or_imprecise_dtypes=True)
+        nc.gpsimd.iota(thr[:, 16:20], pattern=[[8, 4]], base=0, channel_multiplier=0, allow_small_or_imprecise_dtypes=True)
+        ident = keep.tile([P, P], F32, name="ident")
+        make_identity(nc, ident[:])
+        bvrow = keep.tile([P, 256], F32, name="bvrow")
+        nc.gpsimd.memset(bvrow[:], 0.0)
+        nine = keep.tile([P, P], F32, name="nine")
+        nc.gpsimd.memset(nine[:], 9.0)
+        ck = keep.tile([P, 110], F32, name="ck")
+        nc.gpsimd.memset(ck[:, 0:1], 1.0 / 128.0)
+        nc.gpsimd.memset(ck[:, 1:10], 9.0 / 128.0)
+        nc.gpsimd.memset(ck[:, 10:46], 9.0 / 32.0)
+        nc.gpsimd.memset(ck[:, 46:110], 0.5)
+
+        wt = keep.tile([P, 20], F32, name="wt")
+        nc.vector.memset(wt[:, 0:9], 0.5)
+        nc.vector.memset(wt[:, 9:16], 9.0 / 32.0)
+        nc.vector.memset(wt[:, 16:20], 9.0 / 128.0)
+        pm = keep.tile([P, 5, P], F32, name="pm")
+        nc.vector.memset(pm[:], 0.0)
+        nc.vector.memset(pm[:, :, 0:1], 1.0 / 128.0)
+
+        nh = keep.tile([P, 5], F32, name="nh")
+        dge = keep.tile([P, 5, 23], F32, name="dge")
+        hw = keep.tile([P, 5, 2], F32, name="hw")
+        gge = keep.tile([P, 10, 20], F32, name="gge")
+        ind = keep.tile([P, 5, 2, 19], F32, name="ind")
+        rw = keep.tile([P, 5, 19], F32, name="rw")
+
+        def pm_level(tok0, t0, s):
+            nc.vector.tensor_tensor(
+                out=pm[:, :, tok0 : tok0 + s * s].rearrange("p t (a b) -> p t a b", a=s),
+                in0=rw[:, :, t0 : t0 + s].unsqueeze(3).to_broadcast([P, 5, s, s]),
+                in1=ind[:, :, 1, t0 : t0 + s].unsqueeze(2).to_broadcast([P, 5, s, s]),
+                op=ALU.mult,
+            )
+
+        def pm_step(i):
+            if i == 0:
+                nc.vector.tensor_scalar(out=nh[:], in0=nn[:], scalar1=0.5, scalar2=None, op0=ALU.mult)
+            elif i == 1:
+                nc.vector.tensor_tensor(
+                    out=dge[:],
+                    in0=nh[:].unsqueeze(2).to_broadcast([P, 5, 23]),
+                    in1=th24[:].unsqueeze(1).to_broadcast([P, 5, 23]),
+                    op=ALU.is_ge,
+                )
+            elif i == 2:
+                nc.vector.tensor_reduce(out=hw[:, :, 0:1], in_=dge[:], axis=AX.X, op=ALU.add)
+            elif i == 3:
+                nc.vector.scalar_tensor_tensor(out=hw[:, :, 1], in0=hw[:, :, 0], scalar=-24.0, in1=nh[:], op0=ALU.mult, op1=ALU.add)
+            elif i == 4:
+                nc.vector.tensor_tensor(
+                    out=gge[:],
+                    in0=hw[:].rearrange("p a b -> p (a b)").unsqueeze(2).to_broadcast([P, 10, 20]),
+                    in1=thr[:].unsqueeze(1).to_broadcast([P, 10, 20]),
+                    op=ALU.is_ge,
+                )
+            elif i == 5:
+                nc.vector.tensor_tensor(
+                    out=ind[:].rearrange("p a b c -> p (a b) c"), in0=gge[:, :, 0:19], in1=gge[:, :, 1:20], op=ALU.subtract
+                )
+            elif i == 6:
+                nc.vector.tensor_tensor(
+                    out=rw[:], in0=ind[:, :, 0, :], in1=wt[:, 0:19].unsqueeze(1).to_broadcast([P, 5, 19]), op=ALU.mult
+                )
+            elif i == 7:
+                pm_level(46, 0, 8)
+            elif i == 8:
+                pm_level(10, 9, 6)
+            else:
+                pm_level(1, 16, 3)
+
+        bn_std = keep.tile([P, 2], F32, name="bn_std")
+        bn_r = keep.tile([P, 2], F32, name="bn_r")
+        bn_s = keep.tile([P, 2], F32, name="bn_s")
+        bn_d = keep.tile([P, 2], F32, name="bn_d")
+        bn_e = keep.tile([P, 2], F32, name="bn_e")
+        bn_b = keep.tile([P, 2], F32, name="bn_b")
+
+        def bn_step(i):
+            if i == 0:
+                nc.vector.reciprocal(out=bn_r[:], in_=bn_std[:])
+            elif i == 1:
+                nc.vector.tensor_tensor(out=bn_s[:], in0=bn_r[:], in1=bn_in["gk"][:], op=ALU.mult)
+            elif i == 2:
+                nc.vector.tensor_tensor(out=bn_d[:], in0=bn_in["bk"][:], in1=bn_in["mk"][:], op=ALU.subtract)
+            elif i == 3:
+                nc.vector.tensor_tensor(out=bn_e[:], in0=bn_d[:], in1=bn_s[:], op=ALU.mult)
+            else:
+                nc.vector.tensor_tensor(out=bn_b[:], in0=bn_e[:], in1=bn_in["betak"][:], op=ALU.add)
+
+        xw = [keep.tile([P, 2, 4, w], BF16, name="xw%d" % i) for i, (c0, w) in enumerate(PIECES)]
+        xg, xc, xs = [], [], []
+        for c, chunk in enumerate(CHUNKS):
+            w = chunk[1]
+            xg.append(keep.tile([P, 2, w, 4], BF16, name="xg%d" % c, align_bytes=64))
+            xc.append(keep.tile([P, 2, w], U32, name="xc%d" % c, align_bytes=64))
+            xs.append(keep.tile([P, 2, w], U8, name="xs%d" % c, align_bytes=64))
+
+        def widen(on_vector, i, g, planes):
+            for t in planes:
+                if on_vector:
+                    nc.vector.tensor_scalar(
+                        out=xw[i][:, g, t, :], in0=xb[i][:, g, t, :].bitcast(FP8), scalar1=sc[:, g, t : t + 1], scalar2=None, op0=ALU.mult
+                    )
+                else:
+                    nc.scalar.activation(
+                        out=xw[i][:, g, t, :], in_=xb[i][:, g, t, :].bitcast(FP8), func=ACT.Copy, scale=sc[:, g, t : t + 1]
+                    )
+
+        def interleave(c, g):
+            c0, w, paired, i, f0 = CHUNKS[c]
+            nc.vector.tensor_copy(
+                out=xg[c][:, g].rearrange("p (e c i) t -> p e c t i", e=2, i=4),
+                in_=xw[i][:, g, :, f0 : f0 + w].rearrange("p t (c i e) -> p e c t i", i=4, e=2),
+            )
+
+        def interleave_plain(c):
+            c0, w, paired, i, f0 = CHUNKS[c]
+            nc.scalar.copy(out=xg[c][:], in_=xw[i][:, :, :, f0 : f0 + w].rearrange("p g t n -> p g n t"))
+
+        def quantize(c, g):
+            nc.vector.quantize_mx(
+                out=xc[c][:, g, :].bitcast(FP8X4), scales=xs[c][:, g, :], in_=xg[c][:, g].rearrange("p n t -> p (n t)")
+            )
+
+        def quantize_both(c):
+            nc.vector.quantize_mx(
+                out=xc[c][:].rearrange("p g n -> p (g n)").bitcast(FP8X4),
+                scales=xs[c][:].rearrange("p g n -> p (g n)"),
+                in_=xg[c][:].rearrange("p g n t -> p (g n t)"),
+            )
+
+        wgs, wcodes, wscales = [], [], []
+        for nm in ("k", "v"):
+            wgs.append(keep.tile([P, 2048], BF16, name="wg" + nm, align_bytes=64))
+            wcodes.append(keep.tile([P, 2, 256], U32, name="wc" + nm, align_bytes=64))
+            wscales.append(keep.tile([P, 2, 256], U8, name="ws" + nm, align_bytes=64))
+        wkc, wvc = wcodes
+        wks, wvs = wscales
+
+        def turn_weights(i, w_sb):
+            wgw = wgs[i][:].bitcast(F32).rearrange("p (g r c u) -> p g r c u", g=2, r=2, c=P, u=2)
+            for r in range(2):
+                words = w_sb[:, r, :].bitcast(F32)
+                wt_ps = ps_big.tile([P, 2, 2, P], F32, name="big_ps")
+                for g in range(2):
+                    for u in range(2):
+                        nc.tensor.transpose(wt_ps[:, g, u, :], words[:, 256 * g + u : 256 * (g + 1) : 2], ident[:])
+                nc.scalar.copy(out=wgw[:, :, r], in_=wt_ps[:].rearrange("p g u c -> p g c u"))
+
+        def quantize_weights(i):
+            nc.vector.quantize_mx(
+                out=wcodes[i][:].rearrange("p g c -> p (g c)").bitcast(FP8X4),
+                scales=wscales[i][:].rearrange("p g c -> p (g c)"),
+                in_=wgs[i][:],
+            )
+
+        kf = keep.tile([P, 2, NPOS], F32, name="kf")
+        s1 = keep.tile([P, 2, NPOS // 2], F32, name="s1")
+        ks = keep.tile([P, 2, 110], F32, name="ks")
+        acc = keep.tile([P, 2, 3], F32, name="acc")
+        val_ps = ps_val.tile([P, 256], F32, name="val_ps")
+        kf_out = out_0[0].rearrange("(p m) h w -> p m (h w)", m=2)
+        kf_pss, vt_pss, vts = {}, {}, {}
+
+        def mx(out, lc, ls, rc, rs, start, stop):
+            nc.tensor.matmul_mx(
+                out=out, lhsT=lc.bitcast(FP8X4), lhsT_scale=ls, rhs=rc.bitcast(FP8X4), rhs_scale=rs, start=start, stop=stop
+            )
+
+        def shape_of(c):
+            c0, w, paired = CHUNKS[c][0:3]
+            halves = 2 if paired else 1
+            return c0, w, halves, w // halves, w // halves // P
+
+        def mx_kf(c, g):
+            w = CHUNKS[c][1]
+            for m in range(2):
+                if g == 0:
+                    kf_pss[(c, m)] = ps_big.tile([P, w], F32, name="big_ps")
+                mx(
+                    kf_pss[(c, m)][:],
+                    wkc[:, g, m * P : (m + 1) * P],
+                    wks[:, g, m * P : (m + 1) * P],
+                    xc[c][:, g, :],
+                    xs[c][:, g, :],
+                    g == 0,
+                    g == 1,
+                )
+
+        def act_kf(c):
+            c0, w, halves, hwid, subs = shape_of(c)
+            for m in range(2):
+                kf_ps = kf_pss[(c, m)]
+                if halves == 2:
+                    nc.scalar.activation(
+                        out=kf[:, m, c0 : c0 + w].rearrange("p (n e) -> p n e", e=2),
+                        in_=kf_ps[:].rearrange("p (e n) -> p n e", e=2),
+                        func=ACT.Relu,
+                        bias=bn_b[:, m : m + 1],
+                        scale=bn_s[:, m : m + 1],
+                        accum_out=acc[:, m, c : c + 1],
+                    )
+                else:
+                    nc.scalar.activation(
+                        out=kf[:, m, c0 : c0 + w],
+                        in_=kf_ps[:],
+                        func=ACT.Relu,
+                        bias=bn_b[:, m : m + 1],
+                        scale=bn_s[:, m : m + 1],
+                        accum_out=acc[:, m, c : c + 1],
+                    )
+                nc.sync.dma_start(out=kf_out[:, m, c0 : c0 + w], in_=kf[:, m, c0 : c0 + w])
+
+        def mx_vt(c):
+            c0, w, halves, hwid, subs = shape_of(c)
+            vt_ps = ps_vt.tile([P, subs, 256], F32, name="vt_ps")
+            vt_pss[c] = vt_ps
+            for sub in range(subs):
+                for e in range(halves):
+                    cols = slice(e * hwid + sub * P, e * hwid + (sub + 1) * P)
+                    for g in range(2):
+                        mx(
+                            vt_ps[:, sub, :],
+                            xc[c][:, g, cols],
+                            xs[c][:, g, cols],
+                            wvc[:, g, :],
+                            wvs[:, g, :],
+                            e == 0 and g == 0,
+                            e == halves - 1 and g == 1,
+                        )
+
+        def copy_vt(c):
+            subs = shape_of(c)[4]
+            vts[c] = keep.tile([P, subs, 256], F32, name="vt%d" % c)
+            nc.scalar.copy(out=vts[c][:], in_=vt_pss[c][:])
+
+        def pool_val(c):
+            for sub in range(shape_of(c)[4]):
+                tau = 2 * c + sub
+                nc.tensor.matmul(out=val_ps[:], lhsT=pm[:, tau, :], rhs=vts[c][:, sub, :], start=False, stop=(tau == 4))
+
+        def pair_sums(c, m):
+            c0, w = CHUNKS[c][0:2]
+            nc.vector.tensor_tensor(
+                out=s1[:, m, c0 // 2 : (c0 + w) // 2], in0=kf[:, m, c0 : c0 + w : 2], in1=kf[:, m, c0 + 1 : c0 + w : 2], op=ALU.add
+            )
+
+        def bands(tok0, s, a0, a1, m):
+            d = 24 // s
+            nc.vector.tensor_reduce(
+                out=ks[:, m, tok0 + s * a0 : tok0 + s * a1].rearrange("p (a b) -> p a b", b=s),
+                in_=s1[:, m, 24 * d * a0 : 24 * d * a1].rearrange("p (a d b e) -> p a b d e", d=d, b=s, e=d),
+                axis=AX.XY,
+                op=ALU.add,
+            )
+
+        def last_band(tok0, s):
+            d = 24 // s
+            nc.vector.tensor_reduce(
+                out=ks[:, :, tok0 + s * (s - 1) : tok0 + s * s],
+                in_=s1[:, :, 24 * d * (s - 1) : 24 * d * s].rearrange("p m (d b e) -> p m b d e", d=d, b=s, e=d),
+                axis=AX.XY,
+                op=ALU.add,
+            )
+
+        for i in range(4):
+            pm_step(i)
+        widen(True, 0, 0, ALL4)
+        widen(False, 0, 1, ALL4)
+        pm_step(4)
+        interleave(0, 0)
+        pm_step(5)
+        turn_weights(0, wk_sb)
+        interleave(0, 1)
+        pm_step(6)
+        quantize(0, 0)
+        pm_step(7)
+        quantize(0, 1)
+        turn_weights(1, wv_sb)
+        nc.scalar.activation(out=bn_std[:], in_=bn_in["vk"][:], func=ACT.Sqrt, bias=EPS)
+        pm_step(8)
+        quantize_weights(0)
+        bn_step(2)
+        quantize_weights(1)
+        bn_step(0)
+        widen(False, 1, 0, (0, 1))
+        widen(True, 1, 0, (2, 3))
+        bn_step(1)
+        nc.scalar.copy(out=bvrow[0:1, :], in_=bv_sb[0:1, :])
+        widen(False, 1, 1, ALL4)
+        mx_kf(0, 0)
+        mx_kf(0, 1)
+        mx_vt(0)
+        nc.tensor.matmul(out=val_ps[:], lhsT=nine[:], rhs=bvrow[:], start=True, stop=False)
+        interleave(1, 0)
+        bn_step(3)
+        quantize(1, 0)
+        bn_step(4)
+        interleave(1, 1)
+        pm_step(9)
+        quantize(1, 1)
+        interleave_plain(2)
+        act_kf(0)
+        mx_kf(1, 0)
+        mx_kf(1, 1)
+        mx_vt(1)
+        pair_sums(0, 0)
+        quantize_both(2)
+        copy_vt(0)
+        mx_vt(2)
+        mx_kf(2, 0)
+        mx_kf(2, 1)
+        pool_val(0)
+        pair_sums(0, 1)
+        for m in range(2):
+            bands(46, 8, 0, 3, m)
+        for m in range(2):
+            bands(10, 6, 0, 2, m)
+        act_kf(1)
+        copy_vt(1)
+        pool_val(1)
+        for m in range(2):
+            pair_sums(1, m)
+        for m in range(2):
+            bands(46, 8, 3, 7, m)
+        for m in range(2):
+            bands(10, 6, 2, 5, m)
+        copy_vt(2)
+        act_kf(2)
+        pool_val(2)
+        nc.vector.tensor_tensor(out=s1[:, :, 512:576], in0=kf[:, :, 1024:1152:2], in1=kf[:, :, 1025:1152:2], op=ALU.add)
+        nc.vector.tensor_reduce(out=ks[:, :, 0:1], in_=acc[:], axis=AX.X, op=ALU.add)
+        last_band(10, 6)
+        last_band(46, 8)
+        for m in range(2):
+            nc.vector.tensor_reduce(
+                out=ks[:, m, 1:10].rearrange("p (a b) -> p a b", b=3),
+                in_=ks[:, m, 10:46].rearrange("p (a i b j) -> p a b i j", i=2, b=3, j=2),
+                axis=AX.XY,
+                op=ALU.add,
+            )
+        ko = keep.tile([P, 2, 110], F32, name="ko")
+        nc.vector.scalar_tensor_tensor(
+            out=ko[:], in0=ks[:], scalar=1.0 / 9.0, in1=ck[:].unsqueeze(1).to_broadcast([P, 2, 110]), op0=ALU.mult, op1=ALU.mult
+        )
+        nc.sync.dma_start(out=out_1[0].rearrange("(p m) j -> p m j", m=2), in_=ko[:])
+        vo = keep.tile([P, 256], F32, name="vo")
+        nc.scalar.activation(out=vo[:], in_=val_ps[:], func=ACT.Copy, scale=1.0 / 9.0)
+        nc.scalar.dma_start(out=out_2[0], in_=vo[0:110, :])

@@ -416,4 +416,6 @@ def tile_apnb_pa_kernel(tc, feats_bytes, feats_scale, Wk, bk, gk, betak, mk, vk,
         nc.sync.dma_start(out=out_1[0].rearrange("(p m) j -> p m j", m=2), in_=ko[:])
         vo = keep.tile([P, 256], F32, name="vo")
         nc.scalar.activation(out=vo[:], in_=val_ps[:], func=ACT.Copy, scale=1.0 / 9.0)
-        nc.scalar.dma_start(out=out_2[0], in_=vo[0:110, :])
+        for i, (r0, rows) in enumerate(((0, 64), (64, 32), (96, 8), (104, 4), (108, 2))):
+            queue = nc.scalar if i % 2 == 0 else nc.sync
+            queue.dma_start(out=out_2[0][r0 : r0 + rows, :], in_=vo[r0 : r0 + rows, :])

@@ -344,29 +344,30 @@ def tile_apnb_pa_kernel(tc, feats_bytes, feats_scale, Wk, bk, gk, betak, mk, vk,
         interleave(0, 1)
         pm_step(6)
         quantize(0, 0)
-        pm_step(7)
         quantize(0, 1)
         turn_weights(1, wv_sb)
         nc.scalar.activation(out=bn_std[:], in_=bn_in["vk"][:], func=ACT.Sqrt, bias=EPS)
-        pm_step(8)
         quantize_weights(0)
         bn_step(2)
-        quantize_weights(1)
         bn_step(0)
         widen(False, 1, 0, (0, 1))
-        widen(True, 1, 0, (2, 3))
+        widen(True, 1, 0, (2,))
         bn_step(1)
+        widen(True, 1, 0, (3,))
         nc.scalar.copy(out=bvrow[0:1, :], in_=bv_sb[0:1, :])
         widen(False, 1, 1, ALL4)
+        quantize_weights(1)
+        bn_step(3)
         mx_kf(0, 0)
         mx_kf(0, 1)
         mx_vt(0)
         nc.tensor.matmul(out=val_ps[:], lhsT=nine[:], rhs=bvrow[:], start=True, stop=False)
         interleave(1, 0)
-        bn_step(3)
-        quantize(1, 0)
+        pm_step(7)
         bn_step(4)
+        quantize(1, 0)
         interleave(1, 1)
+        pm_step(8)
         pm_step(9)
         quantize(1, 1)
         interleave_plain(2)
@@ -393,22 +394,28 @@ def tile_apnb_pa_kernel(tc, feats_bytes, feats_scale, Wk, bk, gk, betak, mk, vk,
             pair_sums(1, m)
         for m in range(2):
             bands(46, 8, 3, 7, m)
-        for m in range(2):
-            bands(10, 6, 2, 5, m)
+        bands(10, 6, 2, 5, 0)
         copy_vt(2)
         act_kf(2)
         pool_val(2)
         nc.vector.tensor_tensor(out=s1[:, :, 512:576], in0=kf[:, :, 1024:1152:2], in1=kf[:, :, 1025:1152:2], op=ALU.add)
-        nc.vector.tensor_reduce(out=ks[:, :, 0:1], in_=acc[:], axis=AX.X, op=ALU.add)
-        last_band(10, 6)
-        last_band(46, 8)
+        bands(10, 6, 2, 5, 1)
         for m in range(2):
             nc.vector.tensor_reduce(
-                out=ks[:, m, 1:10].rearrange("p (a b) -> p a b", b=3),
-                in_=ks[:, m, 10:46].rearrange("p (a i b j) -> p a b i j", i=2, b=3, j=2),
+                out=ks[:, m, 1:7].rearrange("p (a b) -> p a b", b=3),
+                in_=ks[:, m, 10:34].rearrange("p (a i b j) -> p a b i j", i=2, b=3, j=2),
                 axis=AX.XY,
                 op=ALU.add,
             )
+        last_band(10, 6)
+        last_band(46, 8)
+        nc.vector.tensor_reduce(out=ks[:, :, 0:1], in_=acc[:], axis=AX.X, op=ALU.add)
+        nc.vector.tensor_reduce(
+            out=ks[:, :, 7:10],
+            in_=ks[:, :, 34:46].rearrange("p m (i b j) -> p m b i j", i=2, b=3, j=2),
+            axis=AX.XY,
+            op=ALU.add,
+        )
         ko = keep.tile([P, 2, 110], F32, name="ko")
         nc.vector.scalar_tensor_tensor(
             out=ko[:], in0=ks[:], scalar=1.0 / 9.0, in1=ck[:].unsqueeze(1).to_broadcast([P, 2, 110]), op0=ALU.mult, op1=ALU.mult

@@ -27,10 +27,11 @@ def tile_apnb_pa_kernel(tc, feats_bytes, feats_scale, Wk, bk, gk, betak, mk, vk,
     nc = tc.nc
     with ExitStack() as ctx:
         keep = ctx.enter_context(tc.tile_pool(name="keep", bufs=1))
-        ps_big = ctx.enter_context(tc.psum_pool(name="ps_big", bufs=4))
-        ps_vt = ctx.enter_context(tc.psum_pool(name="ps_vt", bufs=3))
-        ps_val = ctx.enter_context(tc.psum_pool(name="ps_val", bufs=1))
+        ps = ctx.enter_context(tc.psum_pool(name="ps", bufs=1))
         ctx.enter_context(tc.manual_schedule())
+
+        def bank(i):
+            return ps.tile([P, 512], F32, name="bank%d" % i)
 
         fb = feats_bytes[0].rearrange("(g p t) h w -> g p t (h w)", g=2, p=P, t=4)
         sc = keep.tile([P, 2, 4], F32, name="sc")
@@ -52,15 +53,13 @@ def tile_apnb_pa_kernel(tc, feats_bytes, feats_scale, Wk, bk, gk, betak, mk, vk,
         for nm, vec in (("vk", vk), ("gk", gk), ("bk", bk), ("mk", mk), ("betak", betak)):
             bn_in[nm] = keep.tile([P, 2], BF16, name="bn_" + nm)
             nc.sync.dma_start(out=bn_in[nm][:], in_=vec.rearrange("(p m) -> p m", m=2))
-        bv_sb = keep.tile([P, 256], BF16, name="bv_sb")
-        nc.sync.dma_start(out=bv_sb[0:1, :], in_=bv.rearrange("(o c) -> o c", o=1))
 
-        dummy = keep.tile([P, 2], F32, name="dummy")
-        nc.gpsimd.memset(dummy[:, 0:1], 1.0)
-        nc.scalar.activation(out=dummy[:, 1:2], in_=dummy[:, 0:1], func=ACT.Sqrt)
         nn = keep.tile([P, 5], F32, name="nn")
         nc.gpsimd.iota(nn[:, 0:4], pattern=[[256, 4]], base=0, channel_multiplier=2, allow_small_or_imprecise_dtypes=True)
         nc.gpsimd.iota(nn[:, 4:5], pattern=[[0, 1]], base=1024, channel_multiplier=1, allow_small_or_imprecise_dtypes=True)
+        dummy = keep.tile([P, 2], F32, name="dummy")
+        nc.gpsimd.memset(dummy[:, 0:1], 1.0)
+        nc.scalar.activation(out=dummy[:, 1:2], in_=dummy[:, 0:1], func=ACT.Sqrt)
         th24 = keep.tile([P, 23], F32, name="th24")
         nc.gpsimd.iota(th24[:], pattern=[[24, 23]], base=24, channel_multiplier=0, allow_small_or_imprecise_dtypes=True)
         thr = keep.tile([P, 20], F32, name="thr")
@@ -69,9 +68,10 @@ def tile_apnb_pa_kernel(tc, feats_bytes, feats_scale, Wk, bk, gk, betak, mk, vk,
         nc.gpsimd.iota(thr[:, 16:20], pattern=[[8, 4]], base=0, channel_multiplier=0, allow_small_or_imprecise_dtypes=True)
         ident = keep.tile([P, P], F32, name="ident")
         make_identity(nc, ident[:])
-        bvrow = keep.tile([P, 256], F32, name="bvrow")
-        nc.gpsimd.memset(bvrow[:], 0.0)
-        nine = keep.tile([P, P], F32, name="nine")
+        bv_sb = keep.tile([P, 256], BF16, name="bv_sb")
+        nc.gpsimd.memset(bv_sb[:], 0.0)
+        nc.sync.dma_start(out=bv_sb[0:1, :], in_=bv.rearrange("(o c) -> o c", o=1))
+        nine = keep.tile([P, P], BF16, name="nine")
         nc.gpsimd.memset(nine[:], 9.0)
         ck = keep.tile([P, 110], F32, name="ck")
         nc.gpsimd.memset(ck[:, 0:1], 1.0 / 128.0)
@@ -84,7 +84,7 @@ def tile_apnb_pa_kernel(tc, feats_bytes, feats_scale, Wk, bk, gk, betak, mk, vk,
         nc.vector.memset(wt[:, 9:16], 9.0 / 32.0)
         nc.vector.memset(wt[:, 16:20], 9.0 / 128.0)
         pm = keep.tile([P, 5, P], F32, name="pm")
-        nc.vector.memset(pm[:], 0.0)
+        nc.vector.memset(pm[:, :, 110:P], 0.0)
         nc.vector.memset(pm[:, :, 0:1], 1.0 / 128.0)
 
         nh = keep.tile([P, 5], F32, name="nh")
@@ -211,11 +211,12 @@ def tile_apnb_pa_kernel(tc, feats_bytes, feats_scale, Wk, bk, gk, betak, mk, vk,
             wgw = wgs[i][:].bitcast(F32).rearrange("p (g r c u) -> p g r c u", g=2, r=2, c=P, u=2)
             for r in range(2):
                 words = w_sb[:, r, :].bitcast(F32)
-                wt_ps = ps_big.tile([P, 2, 2, P], F32, name="big_ps")
+                wt_ps = bank(2 * i + r)
                 for g in range(2):
                     for u in range(2):
-                        nc.tensor.transpose(wt_ps[:, g, u, :], words[:, 256 * g + u : 256 * (g + 1) : 2], ident[:])
-                nc.scalar.copy(out=wgw[:, :, r], in_=wt_ps[:].rearrange("p g u c -> p g c u"))
+                        col = (2 * g + u) * P
+                        nc.tensor.transpose(wt_ps[:, col : col + P], words[:, 256 * g + u : 256 * (g + 1) : 2], ident[:])
+                nc.scalar.copy(out=wgw[:, :, r], in_=wt_ps[:].rearrange("p (g u c) -> p g c u", g=2, u=2))
 
         def quantize_weights(i):
             nc.vector.quantize_mx(
@@ -228,9 +229,10 @@ def tile_apnb_pa_kernel(tc, feats_bytes, feats_scale, Wk, bk, gk, betak, mk, vk,
         s1 = keep.tile([P, 2, NPOS // 2], F32, name="s1")
         ks = keep.tile([P, 2, 110], F32, name="ks")
         acc = keep.tile([P, 2, 3], F32, name="acc")
-        val_ps = ps_val.tile([P, 256], F32, name="val_ps")
+        val_bank = bank(7)
+        val_ps = val_bank[:, 0:256]
         kf_out = out_0[0].rearrange("(p m) h w -> p m (h w)", m=2)
-        kf_pss, vt_pss, vts = {}, {}, {}
+        kf_pss, vt_pss, vt_banks, vts = {}, {}, {}, {}
 
         def mx(out, lc, ls, rc, rs, start, stop):
             nc.tensor.matmul_mx(
@@ -242,20 +244,30 @@ def tile_apnb_pa_kernel(tc, feats_bytes, feats_scale, Wk, bk, gk, betak, mk, vk,
             halves = 2 if paired else 1
             return c0, w, halves, w // halves, w // halves // P
 
+        def mx_kf_pass(c, g, m):
+            mx(
+                kf_pss[(c, m)],
+                wkc[:, g, m * P : (m + 1) * P],
+                wks[:, g, m * P : (m + 1) * P],
+                xc[c][:, g, :],
+                xs[c][:, g, :],
+                g == 0,
+                g == 1,
+            )
+
         def mx_kf(c, g):
-            w = CHUNKS[c][1]
             for m in range(2):
                 if g == 0:
-                    kf_pss[(c, m)] = ps_big.tile([P, w], F32, name="big_ps")
-                mx(
-                    kf_pss[(c, m)][:],
-                    wkc[:, g, m * P : (m + 1) * P],
-                    wks[:, g, m * P : (m + 1) * P],
-                    xc[c][:, g, :],
-                    xs[c][:, g, :],
-                    g == 0,
-                    g == 1,
-                )
+                    kf_bank = bank(2 * c + m)
+                    kf_pss[(c, m)] = kf_bank[:, 0:512]
+                mx_kf_pass(c, g, m)
+
+        def mx_kf_last():
+            kf_bank = bank(0)
+            for m in range(2):
+                kf_pss[(2, m)] = kf_bank[:, m * P : (m + 1) * P]
+                for g in range(2):
+                    mx_kf_pass(2, g, m)
 
         def act_kf(c):
             c0, w, halves, hwid, subs = shape_of(c)
@@ -264,7 +276,7 @@ def tile_apnb_pa_kernel(tc, feats_bytes, feats_scale, Wk, bk, gk, betak, mk, vk,
                 if halves == 2:
                     nc.scalar.activation(
                         out=kf[:, m, c0 : c0 + w].rearrange("p (n e) -> p n e", e=2),
-                        in_=kf_ps[:].rearrange("p (e n) -> p n e", e=2),
+                        in_=kf_ps.rearrange("p (e n) -> p n e", e=2),
                         func=ACT.Relu,
                         bias=bn_b[:, m : m + 1],
                         scale=bn_s[:, m : m + 1],
@@ -273,7 +285,7 @@ def tile_apnb_pa_kernel(tc, feats_bytes, feats_scale, Wk, bk, gk, betak, mk, vk,
                 else:
                     nc.scalar.activation(
                         out=kf[:, m, c0 : c0 + w],
-                        in_=kf_ps[:],
+                        in_=kf_ps,
                         func=ACT.Relu,
                         bias=bn_b[:, m : m + 1],
                         scale=bn_s[:, m : m + 1],
@@ -281,33 +293,33 @@ def tile_apnb_pa_kernel(tc, feats_bytes, feats_scale, Wk, bk, gk, betak, mk, vk,
                     )
                 nc.sync.dma_start(out=kf_out[:, m, c0 : c0 + w], in_=kf[:, m, c0 : c0 + w])
 
-        def mx_vt(c):
+        def mx_vt(c, sub, gs):
             c0, w, halves, hwid, subs = shape_of(c)
-            vt_ps = ps_vt.tile([P, subs, 256], F32, name="vt_ps")
-            vt_pss[c] = vt_ps
-            for sub in range(subs):
+            for g in gs:
                 for e in range(halves):
                     cols = slice(e * hwid + sub * P, e * hwid + (sub + 1) * P)
-                    for g in range(2):
-                        mx(
-                            vt_ps[:, sub, :],
-                            xc[c][:, g, cols],
-                            xs[c][:, g, cols],
-                            wvc[:, g, :],
-                            wvs[:, g, :],
-                            e == 0 and g == 0,
-                            e == halves - 1 and g == 1,
-                        )
+                    mx(
+                        vt_pss[(c, sub)],
+                        xc[c][:, g, cols],
+                        xs[c][:, g, cols],
+                        wvc[:, g, :],
+                        wvs[:, g, :],
+                        e == 0 and g == 0,
+                        e == halves - 1 and g == 1,
+                    )
 
-        def copy_vt(c):
-            subs = shape_of(c)[4]
-            vts[c] = keep.tile([P, subs, 256], F32, name="vt%d" % c)
-            nc.scalar.copy(out=vts[c][:], in_=vt_pss[c][:])
+        for c in range(3):
+            vts[c] = keep.tile([P, shape_of(c)[4], 256], F32, name="vt%d" % c)
+
+        def copy_vt(c, sub, subs):
+            nc.scalar.copy(
+                out=vts[c][:, sub : sub + subs, :].rearrange("p s n -> p (s n)"), in_=vt_banks[(c, sub)][:, 0 : 256 * subs]
+            )
 
         def pool_val(c):
             for sub in range(shape_of(c)[4]):
                 tau = 2 * c + sub
-                nc.tensor.matmul(out=val_ps[:], lhsT=pm[:, tau, :], rhs=vts[c][:, sub, :], start=False, stop=(tau == 4))
+                nc.tensor.matmul(out=val_ps, lhsT=pm[:, tau, :], rhs=vts[c][:, sub, :], start=False, stop=(tau == 4))
 
         def pair_sums(c, m):
             c0, w = CHUNKS[c][0:2]
@@ -333,16 +345,15 @@ def tile_apnb_pa_kernel(tc, feats_bytes, feats_scale, Wk, bk, gk, betak, mk, vk,
                 op=ALU.add,
             )
 
-        for i in range(4):
+        for i in range(6):
             pm_step(i)
-        widen(True, 0, 0, ALL4)
-        widen(False, 0, 1, ALL4)
-        pm_step(4)
+        for g in range(2):
+            widen(True, 0, g, (0, 1))
+            widen(False, 0, g, (2, 3))
+        pm_step(6)
         interleave(0, 0)
-        pm_step(5)
         turn_weights(0, wk_sb)
         interleave(0, 1)
-        pm_step(6)
         quantize(0, 0)
         quantize(0, 1)
         turn_weights(1, wv_sb)
@@ -354,52 +365,63 @@ def tile_apnb_pa_kernel(tc, feats_bytes, feats_scale, Wk, bk, gk, betak, mk, vk,
         widen(True, 1, 0, (2,))
         bn_step(1)
         widen(True, 1, 0, (3,))
-        nc.scalar.copy(out=bvrow[0:1, :], in_=bv_sb[0:1, :])
         widen(False, 1, 1, ALL4)
         quantize_weights(1)
         bn_step(3)
         mx_kf(0, 0)
         mx_kf(0, 1)
-        mx_vt(0)
-        nc.tensor.matmul(out=val_ps[:], lhsT=nine[:], rhs=bvrow[:], start=True, stop=False)
+        vt_banks[(0, 0)] = bank(4)
+        for sub in range(2):
+            vt_pss[(0, sub)] = vt_banks[(0, 0)][:, 256 * sub : 256 * (sub + 1)]
+            mx_vt(0, sub, (0, 1))
+        nc.tensor.matmul(out=val_ps, lhsT=nine[:], rhs=bv_sb[:], start=True, stop=False)
         interleave(1, 0)
         pm_step(7)
         bn_step(4)
-        quantize(1, 0)
-        interleave(1, 1)
         pm_step(8)
+        quantize(1, 0)
         pm_step(9)
-        quantize(1, 1)
-        interleave_plain(2)
-        act_kf(0)
         mx_kf(1, 0)
-        mx_kf(1, 1)
-        mx_vt(1)
-        pair_sums(0, 0)
-        quantize_both(2)
-        copy_vt(0)
-        mx_vt(2)
-        mx_kf(2, 0)
-        mx_kf(2, 1)
+        for sub in range(2):
+            vt_banks[(1, sub)] = bank(5 + sub)
+            vt_pss[(1, sub)] = vt_banks[(1, sub)][:, 0:256]
+            mx_vt(1, sub, (0,))
+        copy_vt(0, 0, 2)
         pool_val(0)
+        act_kf(0)
+        interleave(1, 1)
+        pair_sums(0, 0)
+        quantize(1, 1)
+        mx_kf(1, 1)
+        for sub in range(2):
+            mx_vt(1, sub, (1,))
+        interleave_plain(2)
         pair_sums(0, 1)
         for m in range(2):
             bands(46, 8, 0, 3, m)
+        quantize_both(2)
         for m in range(2):
             bands(10, 6, 0, 2, m)
+        vt_banks[(2, 0)] = bank(1)
+        vt_pss[(2, 0)] = vt_banks[(2, 0)][:, 0:256]
+        mx_vt(2, 0, (0, 1))
+        mx_kf_last()
         act_kf(1)
-        copy_vt(1)
+        for sub in range(2):
+            copy_vt(1, sub, 1)
         pool_val(1)
         for m in range(2):
             pair_sums(1, m)
         for m in range(2):
             bands(46, 8, 3, 7, m)
         bands(10, 6, 2, 5, 0)
-        copy_vt(2)
+        copy_vt(2, 0, 1)
         act_kf(2)
         pool_val(2)
         nc.vector.tensor_tensor(out=s1[:, :, 512:576], in0=kf[:, :, 1024:1152:2], in1=kf[:, :, 1025:1152:2], op=ALU.add)
         bands(10, 6, 2, 5, 1)
+        last_band(46, 8)
+        last_band(10, 6)
         for m in range(2):
             nc.vector.tensor_reduce(
                 out=ks[:, m, 1:7].rearrange("p (a b) -> p a b", b=3),
@@ -407,8 +429,6 @@ def tile_apnb_pa_kernel(tc, feats_bytes, feats_scale, Wk, bk, gk, betak, mk, vk,
                 axis=AX.XY,
                 op=ALU.add,
             )
-        last_band(10, 6)
-        last_band(46, 8)
         nc.vector.tensor_reduce(out=ks[:, :, 0:1], in_=acc[:], axis=AX.X, op=ALU.add)
         nc.vector.tensor_reduce(
             out=ks[:, :, 7:10],
@@ -417,12 +437,18 @@ def tile_apnb_pa_kernel(tc, feats_bytes, feats_scale, Wk, bk, gk, betak, mk, vk,
             op=ALU.add,
         )
         ko = keep.tile([P, 2, 110], F32, name="ko")
-        nc.vector.scalar_tensor_tensor(
-            out=ko[:], in0=ks[:], scalar=1.0 / 9.0, in1=ck[:].unsqueeze(1).to_broadcast([P, 2, 110]), op0=ALU.mult, op1=ALU.mult
-        )
+        for j0, j1 in ((10, 110), (0, 10)):
+            nc.vector.scalar_tensor_tensor(
+                out=ko[:, :, j0:j1],
+                in0=ks[:, :, j0:j1],
+                scalar=1.0 / 9.0,
+                in1=ck[:, j0:j1].unsqueeze(1).to_broadcast([P, 2, j1 - j0]),
+                op0=ALU.mult,
+                op1=ALU.mult,
+            )
         nc.sync.dma_start(out=out_1[0].rearrange("(p m) j -> p m j", m=2), in_=ko[:])
         vo = keep.tile([P, 256], F32, name="vo")
-        nc.scalar.activation(out=vo[:], in_=val_ps[:], func=ACT.Copy, scale=1.0 / 9.0)
+        nc.scalar.activation(out=vo[:], in_=val_ps, func=ACT.Copy, scale=1.0 / 9.0)
         for i, (r0, rows) in enumerate(((0, 64), (64, 32), (96, 8), (104, 4), (108, 2))):
             queue = nc.scalar if i % 2 == 0 else nc.sync
             queue.dma_start(out=out_2[0][r0 : r0 + rows, :], in_=vo[r0 : r0 + rows, :])

@@ -73,11 +73,6 @@ def tile_apnb_pa_kernel(tc, feats_bytes, feats_scale, Wk, bk, gk, betak, mk, vk,
         nc.sync.dma_start(out=bv_sb[0:1, :], in_=bv.rearrange("(o c) -> o c", o=1))
         nine = keep.tile([P, P], BF16, name="nine")
         nc.gpsimd.memset(nine[:], 9.0)
-        ck = keep.tile([P, 110], F32, name="ck")
-        nc.gpsimd.memset(ck[:, 0:1], 1.0 / 128.0)
-        nc.gpsimd.memset(ck[:, 1:10], 9.0 / 128.0)
-        nc.gpsimd.memset(ck[:, 10:46], 9.0 / 32.0)
-        nc.gpsimd.memset(ck[:, 46:110], 0.5)
 
         wt = keep.tile([P, 20], F32, name="wt")
         nc.vector.memset(wt[:, 0:9], 0.5)
@@ -227,7 +222,9 @@ def tile_apnb_pa_kernel(tc, feats_bytes, feats_scale, Wk, bk, gk, betak, mk, vk,
 
         kf = keep.tile([P, 2, NPOS], F32, name="kf")
         s1 = keep.tile([P, 2, NPOS // 2], F32, name="s1")
-        ks = keep.tile([P, 2, 110], F32, name="ks")
+        ks = {}
+        for s in (1, 3, 6, 8):
+            ks[s] = keep.tile([P, 2, s * s], F32, name="ks%d" % s)
         acc = keep.tile([P, 2, 3], F32, name="acc")
         val_bank = bank(7)
         val_ps = val_bank[:, 0:256]
@@ -327,19 +324,19 @@ def tile_apnb_pa_kernel(tc, feats_bytes, feats_scale, Wk, bk, gk, betak, mk, vk,
                 out=s1[:, m, c0 // 2 : (c0 + w) // 2], in0=kf[:, m, c0 : c0 + w : 2], in1=kf[:, m, c0 + 1 : c0 + w : 2], op=ALU.add
             )
 
-        def bands(tok0, s, a0, a1, m):
+        def bands(s, a0, a1, m):
             d = 24 // s
             nc.vector.tensor_reduce(
-                out=ks[:, m, tok0 + s * a0 : tok0 + s * a1].rearrange("p (a b) -> p a b", b=s),
+                out=ks[s][:, m, s * a0 : s * a1].rearrange("p (a b) -> p a b", b=s),
                 in_=s1[:, m, 24 * d * a0 : 24 * d * a1].rearrange("p (a d b e) -> p a b d e", d=d, b=s, e=d),
                 axis=AX.XY,
                 op=ALU.add,
             )
 
-        def last_band(tok0, s):
+        def last_band(s):
             d = 24 // s
             nc.vector.tensor_reduce(
-                out=ks[:, :, tok0 + s * (s - 1) : tok0 + s * s],
+                out=ks[s][:, :, s * (s - 1) : s * s],
                 in_=s1[:, :, 24 * d * (s - 1) : 24 * d * s].rearrange("p m (d b e) -> p m b d e", d=d, b=s, e=d),
                 axis=AX.XY,
                 op=ALU.add,
@@ -398,10 +395,10 @@ def tile_apnb_pa_kernel(tc, feats_bytes, feats_scale, Wk, bk, gk, betak, mk, vk,
         interleave_plain(2)
         pair_sums(0, 1)
         for m in range(2):
-            bands(46, 8, 0, 3, m)
+            bands(8, 0, 3, m)
         quantize_both(2)
         for m in range(2):
-            bands(10, 6, 0, 2, m)
+            bands(6, 0, 2, m)
         vt_banks[(2, 0)] = bank(1)
         vt_pss[(2, 0)] = vt_banks[(2, 0)][:, 0:256]
         mx_vt(2, 0, (0, 1))
@@ -413,39 +410,25 @@ def tile_apnb_pa_kernel(tc, feats_bytes, feats_scale, Wk, bk, gk, betak, mk, vk,
         for m in range(2):
             pair_sums(1, m)
         for m in range(2):
-            bands(46, 8, 3, 7, m)
-        bands(10, 6, 2, 5, 0)
+            bands(8, 3, 7, m)
+        bands(6, 2, 5, 0)
         copy_vt(2, 0, 1)
         act_kf(2)
         pool_val(2)
         nc.vector.tensor_tensor(out=s1[:, :, 512:576], in0=kf[:, :, 1024:1152:2], in1=kf[:, :, 1025:1152:2], op=ALU.add)
-        bands(10, 6, 2, 5, 1)
-        last_band(46, 8)
-        last_band(10, 6)
-        for m in range(2):
-            nc.vector.tensor_reduce(
-                out=ks[:, m, 1:7].rearrange("p (a b) -> p a b", b=3),
-                in_=ks[:, m, 10:34].rearrange("p (a i b j) -> p a b i j", i=2, b=3, j=2),
-                axis=AX.XY,
-                op=ALU.add,
-            )
-        nc.vector.tensor_reduce(out=ks[:, :, 0:1], in_=acc[:], axis=AX.X, op=ALU.add)
+        bands(6, 2, 5, 1)
+        last_band(6)
+        last_band(8)
+        nc.vector.tensor_reduce(out=ks[1][:], in_=acc[:], axis=AX.X, op=ALU.add)
         nc.vector.tensor_reduce(
-            out=ks[:, :, 7:10],
-            in_=ks[:, :, 34:46].rearrange("p m (i b j) -> p m b i j", i=2, b=3, j=2),
+            out=ks[3][:].rearrange("p m (a b) -> p (m a) b", b=3),
+            in_=ks[6][:].rearrange("p m (a i b j) -> p (m a) b i j", i=2, b=3, j=2),
             axis=AX.XY,
             op=ALU.add,
         )
         ko = keep.tile([P, 2, 110], F32, name="ko")
-        for j0, j1 in ((10, 110), (0, 10)):
-            nc.vector.scalar_tensor_tensor(
-                out=ko[:, :, j0:j1],
-                in0=ks[:, :, j0:j1],
-                scalar=1.0 / 9.0,
-                in1=ck[:, j0:j1].unsqueeze(1).to_broadcast([P, 2, j1 - j0]),
-                op0=ALU.mult,
-                op1=ALU.mult,
-            )
+        for s, tok0 in ((6, 10), (8, 46), (1, 0), (3, 1)):
+            nc.scalar.activation(out=ko[:, :, tok0 : tok0 + s * s], in_=ks[s][:], func=ACT.Copy, scale=float(s * s) / float(NPOS))
         nc.sync.dma_start(out=out_1[0].rearrange("(p m) j -> p m j", m=2), in_=ko[:])
         vo = keep.tile([P, 256], F32, name="vo")
         nc.scalar.activation(out=vo[:], in_=val_ps, func=ACT.Copy, scale=1.0 / 9.0)

@@ -354,6 +354,9 @@ def tile_apnb_pa_kernel(tc, feats_bytes, feats_scale, Wk, bk, gk, betak, mk, vk,
         quantize(0, 0)
         quantize(0, 1)
         turn_weights(1, wv_sb)
+        warm = bank(4)
+        for i in range(3):
+            nc.tensor.matmul(out=warm[:, 0:512], lhsT=nine[:], rhs=wk_sb[:, 0, 0:512], start=True, stop=True)
         nc.scalar.activation(out=bn_std[:], in_=bn_in["vk"][:], func=ACT.Sqrt, bias=EPS)
         quantize_weights(0)
         bn_step(2)

@@ -45,9 +45,13 @@ def tile_apnb_pa_kernel(tc, feats_bytes, feats_scale, Wk, bk, gk, betak, mk, vk,
 
         load_bytes(0)
         wk_sb = keep.tile([P, 2, 1024], BF16, name="wk_sb")
-        nc.sync.dma_start(out=wk_sb[:], in_=Wk.rearrange("(p m) k -> p m k", m=2))
+        wk_rows = Wk.rearrange("(p m) k -> p m k", m=2)
+        for r in range(2):
+            nc.sync.dma_start(out=wk_sb[:, r, :], in_=wk_rows[:, r, :])
         wv_sb = keep.tile([P, 2, 1024], BF16, name="wv_sb")
-        nc.sync.dma_start(out=wv_sb[:], in_=Wv.rearrange("(r p) k -> p r k", r=2))
+        wv_rows = Wv.rearrange("(r p) k -> p r k", r=2)
+        for r in range(2):
+            nc.sync.dma_start(out=wv_sb[:, r, :], in_=wv_rows[:, r, :])
         load_bytes(1)
         bn_in = {}
         for nm, vec in (("vk", vk), ("gk", gk), ("bk", bk), ("mk", mk), ("betak", betak)):

@@ -48,15 +48,20 @@ def tile_apnb_pa_kernel(tc, feats_bytes, feats_scale, Wk, bk, gk, betak, mk, vk,
         wk_rows = Wk.rearrange("(p m) k -> p m k", m=2)
         for r in range(2):
             nc.sync.dma_start(out=wk_sb[:, r, :], in_=wk_rows[:, r, :])
+        bn_in = {}
+
+        def load_vectors(pairs):
+            for nm, vec in pairs:
+                bn_in[nm] = keep.tile([P, 2], BF16, name="bn_" + nm)
+                nc.sync.dma_start(out=bn_in[nm][:], in_=vec.rearrange("(p m) -> p m", m=2))
+
+        load_vectors((("vk", vk),))
         wv_sb = keep.tile([P, 2, 1024], BF16, name="wv_sb")
         wv_rows = Wv.rearrange("(r p) k -> p r k", r=2)
         for r in range(2):
             nc.sync.dma_start(out=wv_sb[:, r, :], in_=wv_rows[:, r, :])
         load_bytes(1)
-        bn_in = {}
-        for nm, vec in (("vk", vk), ("gk", gk), ("bk", bk), ("mk", mk), ("betak", betak)):
-            bn_in[nm] = keep.tile([P, 2], BF16, name="bn_" + nm)
-            nc.sync.dma_start(out=bn_in[nm][:], in_=vec.rearrange("(p m) -> p m", m=2))
+        load_vectors((("bk", bk), ("mk", mk), ("gk", gk), ("betak", betak)))
 
         nn = keep.tile([P, 5], F32, name="nn")
         nc.gpsimd.iota(nn[:, 0:4], pattern=[[256, 4]], base=0, channel_multiplier=2, allow_small_or_imprecise_dtypes=True)
@@ -320,7 +325,7 @@ def tile_apnb_pa_kernel(tc, feats_bytes, feats_scale, Wk, bk, gk, betak, mk, vk,
         def pool_val(c):
             for sub in range(shape_of(c)[4]):
                 tau = 2 * c + sub
-                nc.tensor.matmul(out=val_ps, lhsT=pm[:, tau, :], rhs=vts[c][:, sub, :], start=False, stop=(tau == 4))
+                nc.tensor.matmul(out=val_ps, lhsT=pm[:, tau, :], rhs=vts[c][:, sub, :], start=(tau == 0), stop=(tau == 4))
 
         def pair_sums(c, m):
             c0, w = CHUNKS[c][0:2]
@@ -361,29 +366,29 @@ def tile_apnb_pa_kernel(tc, feats_bytes, feats_scale, Wk, bk, gk, betak, mk, vk,
         warm = bank(4)
         for i in range(3):
             nc.tensor.matmul(out=warm[:, 0:512], lhsT=nine[:], rhs=wk_sb[:, 0, 0:512], start=True, stop=True)
-        nc.scalar.activation(out=bn_std[:], in_=bn_in["vk"][:], func=ACT.Sqrt, bias=EPS)
         quantize_weights(0)
-        bn_step(2)
-        bn_step(0)
         widen(False, 1, 0, (0, 1))
-        widen(True, 1, 0, (2,))
-        bn_step(1)
-        widen(True, 1, 0, (3,))
-        widen(False, 1, 1, ALL4)
+        widen(True, 1, 0, (2, 3))
+        widen(False, 1, 1, (0,))
+        nc.scalar.activation(out=bn_std[:], in_=bn_in["vk"][:], func=ACT.Sqrt, bias=EPS)
+        widen(False, 1, 1, (1, 2))
         quantize_weights(1)
-        bn_step(3)
+        widen(True, 1, 1, (3,))
         mx_kf(0, 0)
         mx_kf(0, 1)
         vt_banks[(0, 0)] = bank(4)
         for sub in range(2):
             vt_pss[(0, sub)] = vt_banks[(0, 0)][:, 256 * sub : 256 * (sub + 1)]
             mx_vt(0, sub, (0, 1))
-        nc.tensor.matmul(out=val_ps, lhsT=nine[:], rhs=bv_sb[:], start=True, stop=False)
         interleave(1, 0)
+        bn_step(2)
+        bn_step(0)
         pm_step(7)
-        bn_step(4)
+        bn_step(1)
         pm_step(8)
+        bn_step(3)
         quantize(1, 0)
+        bn_step(4)
         pm_step(9)
         mx_kf(1, 0)
         for sub in range(2):
@@ -399,6 +404,7 @@ def tile_apnb_pa_kernel(tc, feats_bytes, feats_scale, Wk, bk, gk, betak, mk, vk,
         mx_kf(1, 1)
         for sub in range(2):
             mx_vt(1, sub, (1,))
+        nc.tensor.matmul(out=val_ps, lhsT=nine[:], rhs=bv_sb[:], start=False, stop=False)
         interleave_plain(2)
         pair_sums(0, 1)
         for m in range(2):

@@ -83,6 +83,8 @@ def tile_apnb_pa_kernel(tc, feats_bytes, feats_scale, Wk, bk, gk, betak, mk, vk,
         nine = keep.tile([P, P], BF16, name="nine")
         nc.gpsimd.memset(nine[:], 9.0)
 
+        ones = keep.tile([P, P], F32, name="ones")
+        nc.vector.memset(ones[:], 1.0)
         wt = keep.tile([P, 20], F32, name="wt")
         nc.vector.memset(wt[:, 0:9], 0.5)
         nc.vector.memset(wt[:, 9:16], 9.0 / 32.0)
@@ -358,14 +360,17 @@ def tile_apnb_pa_kernel(tc, feats_bytes, feats_scale, Wk, bk, gk, betak, mk, vk,
             widen(False, 0, g, (2, 3))
         pm_step(6)
         interleave(0, 0)
+        warm = bank(4)
+        for i in range(4):
+            nc.tensor.matmul(out=warm[:, 0:P], lhsT=ones[:], rhs=ones[:], start=True, stop=True)
         turn_weights(0, wk_sb)
         interleave(0, 1)
         quantize(0, 0)
         quantize(0, 1)
         turn_weights(1, wv_sb)
-        warm = bank(4)
-        for i in range(3):
-            nc.tensor.matmul(out=warm[:, 0:512], lhsT=nine[:], rhs=wk_sb[:, 0, 0:512], start=True, stop=True)
+        nc.tensor.matmul(out=warm[:, 0:512], lhsT=nine[:], rhs=wk_sb[:, 0, 0:512], start=True, stop=True)
+        for i in range(2):
+            nc.tensor.matmul(out=warm[:, 0:512], lhsT=nine[:], rhs=wgs[1][:, 512:1024], start=True, stop=True)
         quantize_weights(0)
         widen(False, 1, 0, (0, 1))
         widen(True, 1, 0, (2, 3))

from contextlib import ExitStack

import concourse.mybir as mybir
from concourse.masks import make_identity

F32 = mybir.dt.float32
BF16 = mybir.dt.bfloat16
U32 = mybir.dt.uint32
U8 = mybir.dt.uint8
FP8 = mybir.dt.float8_e4m3fn
FP8X4 = mybir.dt.float8_e4m3fn_x4
ALU = mybir.AluOpType
ACT = mybir.ActivationFunctionType
AX = mybir.AxisListType

P = 128
NPOS = 1152
EPS = 1e-5
FLOPS = 2 * 512 * 1024 * 1152

PIECES = ((0, 512), (512, 640))
CHUNKS = ((0, 512, True, 0, 0), (512, 512, True, 1, 0), (1024, 128, False, 1, 512))
ALL4 = (0, 1, 2, 3)


def tile_apnb_pa_kernel(tc, feats_bytes, feats_scale, Wk, bk, gk, betak, mk, vk, Wv, bv, out_0, out_1, out_2):
    nc = tc.nc
    with ExitStack() as ctx:
        keep = ctx.enter_context(tc.tile_pool(name="keep", bufs=1))
        ps = ctx.enter_context(tc.psum_pool(name="ps", bufs=1))
        ctx.enter_context(tc.manual_schedule())

        def bank(i):
            return ps.tile([P, 512], F32, name="bank%d" % i)

        fb = feats_bytes[0].rearrange("(g p t) h w -> g p t (h w)", g=2, p=P, t=4)
        sc = keep.tile([P, 2, 4], F32, name="sc")
        nc.sync.dma_start(out=sc[:], in_=feats_scale[0].rearrange("(g p t) a b -> p g (t a b)", g=2, p=P, t=4))
        xb = [keep.tile([P, 2, 4, w], U8, name="xb%d" % i) for i, (c0, w) in enumerate(PIECES)]

        def load_bytes(i):
            c0, w = PIECES[i]
            for g in range(2):
                nc.sync.dma_start(out=xb[i][:, g], in_=fb[g][:, :, c0 : c0 + w])

        load_bytes(0)
        wk_sb = keep.tile([P, 2, 1024], BF16, name="wk_sb")
        wk_rows = Wk.rearrange("(p m) k -> p m k", m=2)
        for r in range(2):
            nc.sync.dma_start(out=wk_sb[:, r, :], in_=wk_rows[:, r, :])
        bn_in = {}

        def load_vectors(pairs):
            for nm, vec in pairs:
                bn_in[nm] = keep.tile([P, 2], BF16, name="bn_" + nm)
                nc.sync.dma_start(out=bn_in[nm][:], in_=vec.rearrange("(p m) -> p m", m=2))

        load_vectors((("vk", vk),))
        wv_sb = keep.tile([P, 2, 1024], BF16, name="wv_sb")
        wv_rows = Wv.rearrange("(r p) k -> p r k", r=2)
        for r in range(2):
            nc.sync.dma_start(out=wv_sb[:, r, :], in_=wv_rows[:, r, :])
        load_bytes(1)
        load_vectors((("bk", bk), ("mk", mk), ("gk", gk), ("betak", betak)))

        nn = keep.tile([P, 5], F32, name="nn")
        nc.gpsimd.iota(nn[:, 0:4], pattern=[[256, 4]], base=0, channel_multiplier=2, allow_small_or_imprecise_dtypes=True)
        nc.gpsimd.iota(nn[:, 4:5], pattern=[[0, 1]], base=1024, channel_multiplier=1, allow_small_or_imprecise_dtypes=True)
        dummy = keep.tile([P, 2], F32, name="dummy")
        nc.gpsimd.memset(dummy[:, 0:1], 1.0)
        nc.scalar.activation(out=dummy[:, 1:2], in_=dummy[:, 0:1], func=ACT.Sqrt)
        th24 = keep.tile([P, 23], F32, name="th24")
        nc.gpsimd.iota(th24[:], pattern=[[24, 23]], base=24, channel_multiplier=0, allow_small_or_imprecise_dtypes=True)
        thr = keep.tile([P, 20], F32, name="thr")
        nc.gpsimd.iota(thr[:, 0:9], pattern=[[3, 9]], base=0, channel_multiplier=0, allow_small_or_imprecise_dtypes=True)
        nc.gpsimd.iota(thr[:, 9:16], pattern=[[4, 7]], base=0, channel_multiplier=0, allow_small_or_imprecise_dtypes=True)
        nc.gpsimd.iota(thr[:, 16:20], pattern=[[8, 4]], base=0, channel_multiplier=0, allow_small_or_imprecise_dtypes=True)
        ident = keep.tile([P, P], F32, name="ident")
        make_identity(nc, ident[:])
        bv_sb = keep.tile([P, 256], BF16, name="bv_sb")
        nc.gpsimd.memset(bv_sb[:], 0.0)
        nc.sync.dma_start(out=bv_sb[0:1, :], in_=bv.rearrange("(o c) -> o c", o=1))
        nine = keep.tile([P, P], BF16, name="nine")
        nc.gpsimd.memset(nine[:], 9.0)

        ones = keep.tile([P, P], F32, name="ones")
        nc.vector.memset(ones[:], 1.0)
        wt = keep.tile([P, 20], F32, name="wt")
        nc.vector.memset(wt[:, 0:9], 0.5)
        nc.vector.memset(wt[:, 9:16], 9.0 / 32.0)
        nc.vector.memset(wt[:, 16:20], 9.0 / 128.0)
        pm = keep.tile([P, 5, P], F32, name="pm")
        nc.vector.memset(pm[:, :, 110:P], 0.0)
        nc.vector.memset(pm[:, :, 0:1], 1.0 / 128.0)

        nh = keep.tile([P, 5], F32, name="nh")
        dge = keep.tile([P, 5, 23], F32, name="dge")
        hw = keep.tile([P, 5, 2], F32, name="hw")
        gge = keep.tile([P, 10, 20], F32, name="gge")
        ind = keep.tile([P, 5, 2, 19], F32, name="ind")
        rw = keep.tile([P, 5, 19], F32, name="rw")

        def pm_level(tok0, t0, s):
            nc.vector.tensor_tensor(
                out=pm[:, :, tok0 : tok0 + s * s].rearrange("p t (a b) -> p t a b", a=s),
                in0=rw[:, :, t0 : t0 + s].unsqueeze(3).to_broadcast([P, 5, s, s]),
                in1=ind[:, :, 1, t0 : t0 + s].unsqueeze(2).to_broadcast([P, 5, s, s]),
                op=ALU.mult,
            )

        def pm_step(i):
            if i == 0:
                nc.vector.tensor_scalar(out=nh[:], in0=nn[:], scalar1=0.5, scalar2=None, op0=ALU.mult)
            elif i == 1:
                nc.vector.tensor_tensor(
                    out=dge[:],
                    in0=nh[:].unsqueeze(2).to_broadcast([P, 5, 23]),
                    in1=th24[:].unsqueeze(1).to_broadcast([P, 5, 23]),
                    op=ALU.is_ge,
                )
            elif i == 2:
                nc.vector.tensor_reduce(out=hw[:, :, 0:1], in_=dge[:], axis=AX.X, op=ALU.add)
            elif i == 3:
                nc.vector.scalar_tensor_tensor(out=hw[:, :, 1], in0=hw[:, :, 0], scalar=-24.0, in1=nh[:], op0=ALU.mult, op1=ALU.add)
            elif i == 4:
                nc.vector.tensor_tensor(
                    out=gge[:],
                    in0=hw[:].rearrange("p a b -> p (a b)").unsqueeze(2).to_broadcast([P, 10, 20]),
                    in1=thr[:].unsqueeze(1).to_broadcast([P, 10, 20]),
                    op=ALU.is_ge,
                )
            elif i == 5:
                nc.vector.tensor_tensor(
                    out=ind[:].rearrange("p a b c -> p (a b) c"), in0=gge[:, :, 0:19], in1=gge[:, :, 1:20], op=ALU.subtract
                )
            elif i == 6:
                nc.vector.tensor_tensor(
                    out=rw[:], in0=ind[:, :, 0, :], in1=wt[:, 0:19].unsqueeze(1).to_broadcast([P, 5, 19]), op=ALU.mult
                )
            elif i == 7:
                pm_level(46, 0, 8)
            elif i == 8:
                pm_level(10, 9, 6)
            else:
                pm_level(1, 16, 3)

        bn_std = keep.tile([P, 2], F32, name="bn_std")
        bn_r = keep.tile([P, 2], F32, name="bn_r")
        bn_s = keep.tile([P, 2], F32, name="bn_s")
        bn_d = keep.tile([P, 2], F32, name="bn_d")
        bn_e = keep.tile([P, 2], F32, name="bn_e")
        bn_b = keep.tile([P, 2], F32, name="bn_b")

        def bn_step(i):
            if i == 0:
                nc.vector.reciprocal(out=bn_r[:], in_=bn_std[:])
            elif i == 1:
                nc.vector.tensor_tensor(out=bn_s[:], in0=bn_r[:], in1=bn_in["gk"][:], op=ALU.mult)
            elif i == 2:
                nc.vector.tensor_tensor(out=bn_d[:], in0=bn_in["bk"][:], in1=bn_in["mk"][:], op=ALU.subtract)
            elif i == 3:
                nc.vector.tensor_tensor(out=bn_e[:], in0=bn_d[:], in1=bn_s[:], op=ALU.mult)
            else:
                nc.vector.tensor_tensor(out=bn_b[:], in0=bn_e[:], in1=bn_in["betak"][:], op=ALU.add)

        xw = [keep.tile([P, 2, 4, w], BF16, name="xw%d" % i) for i, (c0, w) in enumerate(PIECES)]
        xg, xc, xs = [], [], []
        for c, chunk in enumerate(CHUNKS):
            w = chunk[1]
            xg.append(keep.tile([P, 2, w, 4], BF16, name="xg%d" % c, align_bytes=64))
            xc.append(keep.tile([P, 2, w], U32, name="xc%d" % c, align_bytes=64))
            xs.append(keep.tile([P, 2, w], U8, name="xs%d" % c, align_bytes=64))

        def widen(on_vector, i, g, planes):
            for t in planes:
                if on_vector:
                    nc.vector.tensor_scalar(
                        out=xw[i][:, g, t, :], in0=xb[i][:, g, t, :].bitcast(FP8), scalar1=sc[:, g, t : t + 1], scalar2=None, op0=ALU.mult
                    )
                else:
                    nc.scalar.activation(
                        out=xw[i][:, g, t, :], in_=xb[i][:, g, t, :].bitcast(FP8), func=ACT.Copy, scale=sc[:, g, t : t + 1]
                    )

        def interleave(c, g):
            c0, w, paired, i, f0 = CHUNKS[c]
            nc.vector.tensor_copy(
                out=xg[c][:, g].rearrange("p (e c i) t -> p e c t i", e=2, i=4),
                in_=xw[i][:, g, :, f0 : f0 + w].rearrange("p t (c i e) -> p e c t i", i=4, e=2),
            )

        def interleave_plain(c):
            c0, w, paired, i, f0 = CHUNKS[c]
            nc.scalar.copy(out=xg[c][:], in_=xw[i][:, :, :, f0 : f0 + w].rearrange("p g t n -> p g n t"))

        def quantize(c, g):
            nc.vector.quantize_mx(
                out=xc[c][:, g, :].bitcast(FP8X4), scales=xs[c][:, g, :], in_=xg[c][:, g].rearrange("p n t -> p (n t)")
            )

        def quantize_both(c):
            nc.vector.quantize_mx(
                out=xc[c][:].rearrange("p g n -> p (g n)").bitcast(FP8X4),
                scales=xs[c][:].rearrange("p g n -> p (g n)"),
                in_=xg[c][:].rearrange("p g n t -> p (g n t)"),
            )

        wgs, wcodes, wscales = [], [], []
        for nm in ("k", "v"):
            wgs.append(keep.tile([P, 2048], BF16, name="wg" + nm, align_bytes=64))
            wcodes.append(keep.tile([P, 2, 256], U32, name="wc" + nm, align_bytes=64))
            wscales.append(keep.tile([P, 2, 256], U8, name="ws" + nm, align_bytes=64))
        wkc, wvc = wcodes
        wks, wvs = wscales

        def turn_weights(i, w_sb):
            wgw = wgs[i][:].bitcast(F32).rearrange("p (g r c u) -> p g r c u", g=2, r=2, c=P, u=2)
            for r in range(2):
                words = w_sb[:, r, :].bitcast(F32)
                wt_ps = bank(2 * i + r)
                for g in range(2):
                    for u in range(2):
                        col = (2 * g + u) * P
                        nc.tensor.transpose(wt_ps[:, col : col + P], words[:, 256 * g + u : 256 * (g + 1) : 2], ident[:])
                nc.scalar.copy(out=wgw[:, :, r], in_=wt_ps[:].rearrange("p (g u c) -> p g c u", g=2, u=2))

        def quantize_weights(i):
            nc.vector.quantize_mx(
                out=wcodes[i][:].rearrange("p g c -> p (g c)").bitcast(FP8X4),
                scales=wscales[i][:].rearrange("p g c -> p (g c)"),
                in_=wgs[i][:],
            )

        kf = keep.tile([P, 2, NPOS], F32, name="kf")
        s1 = keep.tile([P, 2, NPOS // 2], F32, name="s1")
        ks = {}
        for s in (1, 3, 6, 8):
            ks[s] = keep.tile([P, 2, s * s], F32, name="ks%d" % s)
        acc = keep.tile([P, 2, 3], F32, name="acc")
        val_bank = bank(7)
        val_ps = val_bank[:, 0:256]
        kf_out = out_0[0].rearrange("(p m) h w -> p m (h w)", m=2)
        kf_pss, vt_pss, vt_banks, vts = {}, {}, {}, {}

        def mx(out, lc, ls, rc, rs, start, stop):
            nc.tensor.matmul_mx(
                out=out, lhsT=lc.bitcast(FP8X4), lhsT_scale=ls, rhs=rc.bitcast(FP8X4), rhs_scale=rs, start=start, stop=stop
            )

        def shape_of(c):
            c0, w, paired = CHUNKS[c][0:3]
            halves = 2 if paired else 1
            return c0, w, halves, w // halves, w // halves // P

        def mx_kf_pass(c, g, m):
            mx(
                kf_pss[(c, m)],
                wkc[:, g, m * P : (m + 1) * P],
                wks[:, g, m * P : (m + 1) * P],
                xc[c][:, g, :],
                xs[c][:, g, :],
                g == 0,
                g == 1,
            )

        def mx_kf(c, g):
            for m in range(2):
                if g == 0:
                    kf_bank = bank(2 * c + m)
                    kf_pss[(c, m)] = kf_bank[:, 0:512]
                mx_kf_pass(c, g, m)

        def mx_kf_last():
            kf_bank = bank(0)
            for m in range(2):
                kf_pss[(2, m)] = kf_bank[:, m * P : (m + 1) * P]
                for g in range(2):
                    mx_kf_pass(2, g, m)

        def act_kf(c):
            c0, w, halves, hwid, subs = shape_of(c)
            for m in range(2):
                kf_ps = kf_pss[(c, m)]
                if halves == 2:
                    nc.scalar.activation(
                        out=kf[:, m, c0 : c0 + w].rearrange("p (n e) -> p n e", e=2),
                        in_=kf_ps.rearrange("p (e n) -> p n e", e=2),
                        func=ACT.Relu,
                        bias=bn_b[:, m : m + 1],
                        scale=bn_s[:, m : m + 1],
                        accum_out=acc[:, m, c : c + 1],
                    )
                else:
                    nc.scalar.activation(
                        out=kf[:, m, c0 : c0 + w],
                        in_=kf_ps,
                        func=ACT.Relu,
                        bias=bn_b[:, m : m + 1],
                        scale=bn_s[:, m : m + 1],
                        accum_out=acc[:, m, c : c + 1],
                    )
                nc.sync.dma_start(out=kf_out[:, m, c0 : c0 + w], in_=kf[:, m, c0 : c0 + w])

        def mx_vt(c, sub, gs):
            c0, w, halves, hwid, subs = shape_of(c)
            for g in gs:
                for e in range(halves):
                    cols = slice(e * hwid + sub * P, e * hwid + (sub + 1) * P)
                    mx(
                        vt_pss[(c, sub)],
                        xc[c][:, g, cols],
                        xs[c][:, g, cols],
                        wvc[:, g, :],
                        wvs[:, g, :],
                        e == 0 and g == 0,
                        e == halves - 1 and g == 1,
                    )

        for c in range(3):
            vts[c] = keep.tile([P, shape_of(c)[4], 256], F32, name="vt%d" % c)

        def copy_vt(c, sub, subs):
            nc.scalar.copy(
                out=vts[c][:, sub : sub + subs, :].rearrange("p s n -> p (s n)"), in_=vt_banks[(c, sub)][:, 0 : 256 * subs]
            )

        def pool_val(c):
            for sub in range(shape_of(c)[4]):
                tau = 2 * c + sub
                nc.tensor.matmul(out=val_ps, lhsT=pm[:, tau, :], rhs=vts[c][:, sub, :], start=(tau == 0), stop=(tau == 4))

        def pair_sums(c, m):
            c0, w = CHUNKS[c][0:2]
            nc.vector.tensor_tensor(
                out=s1[:, m, c0 // 2 : (c0 + w) // 2], in0=kf[:, m, c0 : c0 + w : 2], in1=kf[:, m, c0 + 1 : c0 + w : 2], op=ALU.add
            )

        def bands(s, a0, a1, m):
            d = 24 // s
            nc.vector.tensor_reduce(
                out=ks[s][:, m, s * a0 : s * a1].rearrange("p (a b) -> p a b", b=s),
                in_=s1[:, m, 24 * d * a0 : 24 * d * a1].rearrange("p (a d b e) -> p a b d e", d=d, b=s, e=d),
                axis=AX.XY,
                op=ALU.add,
            )

        def last_band(s):
            d = 24 // s
            nc.vector.tensor_reduce(
                out=ks[s][:, :, s * (s - 1) : s * s],
                in_=s1[:, :, 24 * d * (s - 1) : 24 * d * s].rearrange("p m (d b e) -> p m b d e", d=d, b=s, e=d),
                axis=AX.XY,
                op=ALU.add,
            )

        for i in range(6):
            pm_step(i)
        for g in range(2):
            widen(True, 0, g, (0, 1))
            widen(False, 0, g, (2, 3))
        pm_step(6)
        interleave(0, 0)
        warm = bank(4)
        for i in range(4):
            nc.tensor.matmul(out=warm[:, 0:P], lhsT=ones[:], rhs=ones[:], start=True, stop=True)
        turn_weights(0, wk_sb)
        interleave(0, 1)
        quantize(0, 0)
        quantize(0, 1)
        turn_weights(1, wv_sb)
        nc.tensor.matmul(out=warm[:, 0:512], lhsT=nine[:], rhs=wk_sb[:, 0, 0:512], start=True, stop=True)
        for i in range(2):
            nc.tensor.matmul(out=warm[:, 0:512], lhsT=nine[:], rhs=wgs[1][:, 512:1024], start=True, stop=True)
        quantize_weights(0)
        widen(False, 1, 0, (0, 1))
        widen(True, 1, 0, (2, 3))
        widen(False, 1, 1, (0,))
        nc.scalar.activation(out=bn_std[:], in_=bn_in["vk"][:], func=ACT.Sqrt, bias=EPS)
        widen(False, 1, 1, (1, 2))
        quantize_weights(1)
        widen(True, 1, 1, (3,))
        mx_kf(0, 0)
        mx_kf(0, 1)
        vt_banks[(0, 0)] = bank(4)
        for sub in range(2):
            vt_pss[(0, sub)] = vt_banks[(0, 0)][:, 256 * sub : 256 * (sub + 1)]
            mx_vt(0, sub, (0, 1))
        interleave(1, 0)
        bn_step(2)
        bn_step(0)
        pm_step(7)
        bn_step(1)
        pm_step(8)
        bn_step(3)
        quantize(1, 0)
        bn_step(4)
        pm_step(9)
        mx_kf(1, 0)
        for sub in range(2):
            vt_banks[(1, sub)] = bank(5 + sub)
            vt_pss[(1, sub)] = vt_banks[(1, sub)][:, 0:256]
            mx_vt(1, sub, (0,))
        copy_vt(0, 0, 2)
        pool_val(0)
        act_kf(0)
        interleave(1, 1)
        pair_sums(0, 0)
        quantize(1, 1)
        mx_kf(1, 1)
        for sub in range(2):
            mx_vt(1, sub, (1,))
        nc.tensor.matmul(out=val_ps, lhsT=nine[:], rhs=bv_sb[:], start=False, stop=False)
        interleave_plain(2)
        pair_sums(0, 1)
        for m in range(2):
            bands(8, 0, 3, m)
        quantize_both(2)
        for m in range(2):
            bands(6, 0, 2, m)
        vt_banks[(2, 0)] = bank(1)
        vt_pss[(2, 0)] = vt_banks[(2, 0)][:, 0:256]
        mx_vt(2, 0, (0, 1))
        mx_kf_last()
        act_kf(1)
        for sub in range(2):
            copy_vt(1, sub, 1)
        pool_val(1)
        for m in range(2):
            pair_sums(1, m)
        for m in range(2):
            bands(8, 3, 7, m)
        bands(6, 2, 5, 0)
        copy_vt(2, 0, 1)
        act_kf(2)
        pool_val(2)
        nc.vector.tensor_tensor(out=s1[:, :, 512:576], in0=kf[:, :, 1024:1152:2], in1=kf[:, :, 1025:1152:2], op=ALU.add)
        bands(6, 2, 5, 1)
        last_band(6)
        last_band(8)
        nc.vector.tensor_reduce(out=ks[1][:], in_=acc[:], axis=AX.X, op=ALU.add)
        nc.vector.tensor_reduce(
            out=ks[3][:].rearrange("p m (a b) -> p (m a) b", b=3),
            in_=ks[6][:].rearrange("p m (a i b j) -> p (m a) b i j", i=2, b=3, j=2),
            axis=AX.XY,
            op=ALU.add,
        )
        ko = keep.tile([P, 2, 110], F32, name="ko")
        for s, tok0 in ((6, 10), (8, 46), (1, 0), (3, 1)):
            nc.scalar.activation(out=ko[:, :, tok0 : tok0 + s * s], in_=ks[s][:], func=ACT.Copy, scale=float(s * s) / float(NPOS))
        nc.sync.dma_start(out=out_1[0].rearrange("(p m) j -> p m j", m=2), in_=ko[:])
        vo = keep.tile([P, 256], F32, name="vo")
        nc.scalar.activation(out=vo[:], in_=val_ps, func=ACT.Copy, scale=1.0 / 9.0)
        for i, (r0, rows) in enumerate(((0, 64), (64, 32), (96, 8), (104, 4), (108, 2))):
            queue = nc.scalar if i % 2 == 0 else nc.sync
            queue.dma_start(out=out_2[0][r0 : r0 + rows, :], in_=vo[r0 : r0 + rows, :])
